import numpy as np
import ml_dtypes


def mxq(x, axis, fmt="e4m3"):
    dtype, down = {"e4m3": (ml_dtypes.float8_e4m3fn, 7), "e5m2": (ml_dtypes.float8_e5m2, 14)}[fmt]
    v = np.moveaxis(np.asarray(x, np.float32).astype(ml_dtypes.bfloat16).astype(np.float64), axis, -1)
    blocks = v.reshape(v.shape[:-1] + (-1, 32))
    amax = np.abs(blocks).max(-1, keepdims=True)
    byte = np.maximum(np.where(amax > 0, np.frexp(amax)[1] - 1 + 127, 0) - down, 1)
    scale = np.exp2(byte - 127.0)
    codes = (blocks / scale).astype(np.float32).astype(dtype).astype(np.float64)
    return np.moveaxis((codes * scale).reshape(v.shape), -1, axis)


WIDE = False


def mx_kscale(k):
    if not WIDE:
        return np.ones(k)
    levels = np.array([10, -10, 5, -5, 0])
    a = np.random.permutation(np.resize(levels, k // 512 * 4)).reshape(k // 512, 4)
    idx = np.arange(k)
    return np.exp2(a[idx // 512, idx % 128 // 32])


BF16 = ml_dtypes.bfloat16


def bf(x):
    return np.asarray(x, np.float32).astype(BF16)


def f64(x):
    return np.asarray(x).astype(np.float64)


E2M1 = np.array([0.0, 0.5, 1.0, 1.5, 2.0, 3.0, 4.0, 6.0, -0.0, -0.5, -1.0, -1.5, -2.0, -3.0, -4.0, -6.0])


def pack_weight(w, fmt):
    k, n = w.shape
    w = f64(bf(w)).reshape(k // 32, 32, n)
    amax = np.abs(w).max(1)
    if fmt == "e4m3":
        byte = np.frexp(amax)[1] - 1 + 127 - 7
    else:
        mant, ex = np.frexp(amax / 6.0)
        byte = np.where(mant > 0.5, ex, ex - 1) + 127
    byte = np.clip(np.where(amax > 0, byte, 1), 1, 254)
    scaled = (w * np.exp2(127.0 - byte)[:, None, :]).reshape(k, n).astype(np.float32)
    by_word = np.ascontiguousarray(scaled.reshape(k // 512, 128, 4, n).transpose(0, 1, 3, 2))
    if fmt == "e4m3":
        words = by_word.astype(ml_dtypes.float8_e4m3fn).view(np.uint8)
    else:
        c = by_word.astype(ml_dtypes.float4_e2m1fn).view(np.uint8) & 0xF
        words = c[..., 0::2] | (c[..., 1::2] << 4)
    return np.ascontiguousarray(words), np.ascontiguousarray(byte.astype(np.uint8).reshape(k // 512, 16, n))


def unpack_weight(words, scales, fmt):
    g, p, n, _ = words.shape
    if fmt == "e4m3":
        vals = np.ascontiguousarray(words).view(ml_dtypes.float8_e4m3fn).astype(np.float64)
    else:
        nib = np.empty((g, p, n, 4), np.uint8)
        nib[..., 0::2] = words & 0xF
        nib[..., 1::2] = words >> 4
        vals = E2M1[nib]
    vals = vals * np.repeat(np.exp2(scales.astype(np.float64) - 127.0), 8, axis=1)[..., None]
    return vals.transpose(0, 1, 3, 2).reshape(g * 512, n)

def pack4(w):
    words, scales = pack_weight(w, "e2m1")
    return words.reshape(words.shape[0], 128, -1), scales


def unpack4(words, scales):
    return unpack_weight(words.reshape(words.shape[0], 128, -1, 2), scales, "e2m1")


B, H = 8192, 256
K = 2 * H
G = 4 * H


def sigmoid(v):
    return 1.0 / (1.0 + np.exp(-v))


def setup_inputs():
    s = mx_kscale(K)
    x = bf(np.random.standard_normal((B, H)) * s[:H])
    h_prev = bf(np.random.standard_normal((B, H)) * s[H:])
    c_prev = bf(np.random.standard_normal((B, H)))
    is_rnn = bf(np.random.random((B, 1)))
    words, scales = pack4(np.random.standard_normal((K, G)) / np.sqrt(K) / s[:, None])
    b = bf(np.random.standard_normal(G) * 0.3)
    return {"x": x,
            "h_prev": h_prev,
            "c_prev": c_prev,
            "is_rnn": is_rnn,
            "W_words": words,
            "W_scales": scales,
            "b": b}


def reference(x, h_prev, c_prev, is_rnn, W_words, W_scales, b):
    c_prev, m = f64(c_prev), f64(is_rnn)
    xh = np.concatenate([f64(x), f64(h_prev)], axis=1)
    gates = (mxq(xh, 1, "e4m3") @ unpack4(W_words, W_scales)) + f64(b)
    i = sigmoid(gates[:, :H])
    f = sigmoid(gates[:, H:2 * H])
    g = np.tanh(gates[:, 2 * H:3 * H])
    o = sigmoid(gates[:, 3 * H:])
    c = f * c_prev + i * g
    c = c * m + c_prev * (1.0 - m)
    o = o * m + (1.0 - m)
    return c, o

@@ -1,0 +1,236 @@
+from contextlib import ExitStack
+
+import concourse.mybir as mybir
+from concourse.masks import make_identity
+
+F32 = mybir.dt.float32
+BF16 = mybir.dt.bfloat16
+I32 = mybir.dt.int32
+U32 = mybir.dt.uint32
+U8 = mybir.dt.uint8
+FP8X4 = mybir.dt.float8_e4m3fn_x4
+FP4X4 = mybir.dt.float4_e2m1fn_x4
+ACT = mybir.ActivationFunctionType
+ALU = mybir.AluOpType
+
+P = 128
+B = 8192
+H = 256
+K = 2 * H
+GATES = 4 * H
+H_BLOCKS = H // P
+GATE_I, GATE_F, GATE_G, GATE_O = 0, 1, 2, 3
+ROW_TILES = B // P
+GROUP = 4
+GROUP_ROWS = GROUP * P
+GROUPS = ROW_TILES // GROUP
+HALF = GROUP // 2
+PREFETCH = 3
+
+FLOPS = 2 * B * K * GATES
+
+
+def tile_bag_lstm_pa_t_kernel(tc, x, h_prev, c_prev, is_rnn, W_words, W_scales, b, out_0, out_1):
+    nc = tc.nc
+
+    x_rows = x.rearrange("(p t) k -> p t k", t=ROW_TILES)
+    h_rows = h_prev.rearrange("(p t) k -> p t k", t=ROW_TILES)
+    c_prev_rows = c_prev.rearrange("(p t) k -> p t k", t=ROW_TILES)
+    c_rows = out_0.rearrange("(p t) k -> p t k", t=ROW_TILES)
+    o_rows = out_1.rearrange("(p t) k -> p t k", t=ROW_TILES)
+
+    with ExitStack() as stack:
+        const = stack.enter_context(tc.tile_pool(name="const", bufs=1))
+        xh_pool = stack.enter_context(tc.tile_pool(name="xh", bufs=PREFETCH + 2))
+        c_prev_pool = stack.enter_context(tc.tile_pool(name="c_prev", bufs=PREFETCH + 5))
+        work = stack.enter_context(tc.tile_pool(name="work", bufs=2))
+        result = stack.enter_context(tc.tile_pool(name="result", bufs=3))
+        gates_psum = stack.enter_context(tc.psum_pool(name="gates_psum", bufs=4))
+        xh_psum = stack.enter_context(tc.psum_pool(name="xh_psum", bufs=1))
+        fo_psum = stack.enter_context(tc.psum_pool(name="fo_psum", bufs=2))
+        ig_psum = stack.enter_context(tc.psum_pool(name="ig_psum", bufs=1))
+        stack.enter_context(tc.manual_schedule())
+
+        xh = {}
+        c_old = {}
+        grouped = {}
+        codes = {}
+        scales = {}
+        gate_t = {}
+        ig_t = {}
+        blend = {}
+        kept = {}
+        c_new = {}
+
+        def load_inputs(g):
+            tiles = slice(g * GROUP, (g + 1) * GROUP)
+            xh[g] = xh_pool.tile([P, GROUP, K], BF16, name="xh")
+            nc.sync.dma_start(out=xh[g][:, :, 0:H], in_=x_rows[:, tiles, :])
+            nc.sync.dma_start(out=xh[g][:, :, H:K], in_=h_rows[:, tiles, :])
+            c_old[g] = c_prev_pool.tile([P, GROUP, H], BF16, name="c_old")
+            nc.sync.dma_start(out=c_old[g][:], in_=c_prev_rows[:, tiles, :])
+
+        b_rows = const.tile([P, P], BF16)
+        nc.vector.memset(b_rows[:], 0.0)
+        nc.sync.dma_start(out=b_rows[0 : GATES // P, :], in_=b.rearrange("(r c) -> r c", c=P))
+        m_bf16 = const.tile([P, ROW_TILES], BF16)
+        nc.sync.dma_start(out=m_bf16[:], in_=is_rnn.rearrange("(p t) o -> p (t o)", t=ROW_TILES))
+        load_inputs(0)
+
+        w_words = const.tile([P, 2 * GATES], U8, align_bytes=64)
+        nc.sync.dma_start(out=w_words[:].bitcast(I32), in_=W_words[0].bitcast(I32))
+        w_scales = const.tile([P, GATES], U8, align_bytes=64)
+        nc.vector.memset(w_scales[:].bitcast(I32), 0)
+        for quadrant in range(4):
+            nc.sync.dma_start(
+                out=w_scales[32 * quadrant : 32 * quadrant + 4, :].bitcast(I32),
+                in_=W_scales[0, 4 * quadrant : 4 * quadrant + 4, :].bitcast(I32),
+            )
+        for g in range(1, PREFETCH):
+            load_inputs(g)
+
+        ident = const.tile([P, P], F32)
+        make_identity(nc, ident[:])
+
+        warm = const.tile([P, 1], F32)
+        nc.vector.memset(warm[:], 0.0)
+        nc.scalar.activation(out=warm[:], in_=warm[:], func=ACT.Sigmoid)
+
+        b_rows_f32 = const.tile([P, P], F32)
+        nc.vector.tensor_copy(out=b_rows_f32[:], in_=b_rows[:])
+        b_columns = ig_psum.tile([P, P], F32, tag="ig")
+        nc.tensor.transpose(b_columns[:], b_rows_f32[:], ident[:])
+        bias = const.tile([P, GATES // P], F32)
+        nc.vector.tensor_copy(out=bias[:], in_=b_columns[:, 0 : GATES // P])
+
+        m = const.tile([P, ROW_TILES], F32)
+        nc.vector.tensor_copy(out=m[:], in_=m_bf16[:])
+        one_minus_m = const.tile([P, ROW_TILES], F32)
+        nc.vector.tensor_scalar(
+            out=one_minus_m[:], in0=m_bf16[:], scalar1=-1.0, scalar2=1.0, op0=ALU.mult, op1=ALU.add
+        )
+
+        def transpose_xh(g, half):
+            if half == 0:
+                if g + PREFETCH < GROUPS:
+                    load_inputs(g + PREFETCH)
+                grouped[g] = work.tile([P, GROUP, P, 4], BF16, name="grouped", align_bytes=64)
+            words = xh[g][:].bitcast(F32)
+            bank = xh_psum.tile([P, HALF, 2, P], F32, tag="xh_t")
+            for j in range(HALF):
+                for u in range(2):
+                    nc.tensor.transpose(bank[:, j, u, :], words[:, half * HALF + j, u : K // 2 : 2], ident[:])
+            target = grouped[g][:].bitcast(F32)[:, half * HALF : (half + 1) * HALF, :, :]
+            source = bank[:].rearrange("p j u r -> p j r u")
+            if half == 0:
+                nc.scalar.copy(out=target, in_=source)
+            else:
+                nc.vector.tensor_copy(out=target, in_=source)
+
+        def quantise_xh(g):
+            codes[g] = work.tile([P, GROUP_ROWS], U32, name="codes", align_bytes=64)
+            scales[g] = work.tile([P, GROUP_ROWS], U8, name="scales", align_bytes=64)
+            nc.vector.quantize_mx(
+                out=codes[g][:].bitcast(FP8X4),
+                scales=scales[g][:],
+                in_=grouped[g][:].rearrange("p j r t -> p (j r t)"),
+            )
+
+        def compute_gates(g, gates):
+            for gate in gates:
+                gate_t[g, gate] = work.tile([P, H_BLOCKS, GROUP_ROWS], F32, name="gate_t%d" % gate)
+                for hb in range(H_BLOCKS):
+                    block = gate * H_BLOCKS + hb
+                    sums = gates_psum.tile([P, GROUP_ROWS], F32, tag="sums")
+                    nc.tensor.matmul_mx(
+                        out=sums[:],
+                        lhsT=w_words[:, 2 * P * block : 2 * P * (block + 1)].bitcast(FP4X4),
+                        lhsT_scale=w_scales[:, P * block : P * (block + 1)],
+                        rhs=codes[g][:].bitcast(FP8X4),
+                        rhs_scale=scales[g][:],
+                        start=True,
+                        stop=True,
+                    )
+                    nc.scalar.activation(
+                        out=gate_t[g, gate][:, hb, :],
+                        in_=sums[:],
+                        func=ACT.Tanh if gate == GATE_G else ACT.Sigmoid,
+                        bias=bias[:, block : block + 1],
+                        scale=1.0,
+                    )
+
+        def multiply_i_g(g):
+            ig_t[g] = work.tile([P, H_BLOCKS, GROUP_ROWS], F32, name="ig_t")
+            nc.gpsimd.tensor_tensor(out=ig_t[g][:], in0=gate_t[g, GATE_I][:], in1=gate_t[g, GATE_G][:], op=ALU.mult)
+
+        def transpose_back(bank_columns, values_t, j):
+            for hb in range(H_BLOCKS):
+                nc.tensor.transpose(
+                    bank_columns[:, hb * P : (hb + 1) * P], values_t[:, hb, j * P : (j + 1) * P], ident[:]
+                )
+
+        def blend_f_o(g, half):
+            if half == 0:
+                blend[g] = result.tile([P, 2, GROUP, H], F32, name="blend")
+                kept[g] = result.tile([P, GROUP, H], F32, name="kept")
+            for j in range(half * HALF, (half + 1) * HALF):
+                t = g * GROUP + j
+                bank = fo_psum.tile([P, 2, H], F32, tag="fo")
+                transpose_back(bank[:, 0, :], gate_t[g, GATE_F], j)
+                transpose_back(bank[:, 1, :], gate_t[g, GATE_O], j)
+                nc.vector.tensor_scalar(
+                    out=blend[g][:, :, j, :],
+                    in0=bank[:],
+                    scalar1=m[:, t : t + 1],
+                    scalar2=one_minus_m[:, t : t + 1],
+                    op0=ALU.mult,
+                    op1=ALU.add,
+                )
+            tiles = slice(half * HALF, (half + 1) * HALF)
+            nc.gpsimd.tensor_tensor(
+                out=kept[g][:, tiles, :], in0=blend[g][:, 0, tiles, :], in1=c_old[g][:, tiles, :], op=ALU.mult
+            )
+            if half == 1:
+                nc.sync.dma_start(out=o_rows[:, g * GROUP : (g + 1) * GROUP, :], in_=blend[g][:, 1, :, :])
+
+        def finish_c(g, half):
+            if half == 0:
+                c_new[g] = result.tile([P, GROUP, H], F32, name="c_new")
+            bank = ig_psum.tile([P, HALF, H], F32, tag="ig")
+            for jj in range(HALF):
+                transpose_back(bank[:, jj, :], ig_t[g], half * HALF + jj)
+            for jj in range(HALF):
+                j = half * HALF + jj
+                t = g * GROUP + j
+                nc.vector.scalar_tensor_tensor(
+                    out=c_new[g][:, j, :],
+                    in0=bank[:, jj, :],
+                    scalar=m[:, t : t + 1],
+                    in1=kept[g][:, j, :],
+                    op0=ALU.mult,
+                    op1=ALU.add,
+                )
+            if half == 1:
+                nc.sync.dma_start(out=c_rows[:, g * GROUP : (g + 1) * GROUP, :], in_=c_new[g][:])
+
+        XH_LEAD = 4
+        FO_LAG = 1
+        IG_LAG = 3
+        for step in range(-XH_LEAD, 2 * GROUPS + IG_LAG):
+            g, part = divmod(step, 2)
+            if part == 0 and 0 <= g - 1 < GROUPS:
+                multiply_i_g(g - 1)
+            if 0 <= g < GROUPS:
+                compute_gates(g, (GATE_F, GATE_O) if part == 0 else (GATE_I, GATE_G))
+            g, half = divmod(step - FO_LAG, 2)
+            if 0 <= g < GROUPS:
+                blend_f_o(g, half)
+            g, half = divmod(step + XH_LEAD - 2, 2)
+            if half == 0 and 0 <= g < GROUPS:
+                quantise_xh(g)
+            g, half = divmod(step - IG_LAG, 2)
+            if 0 <= g < GROUPS:
+                finish_c(g, half)
+            g, half = divmod(step + XH_LEAD, 2)
+            if 0 <= g < GROUPS:
+                transpose_xh(g, half)

@@ -123,9 +123,9 @@ def tile_bag_lstm_pa_t_kernel(tc, x, h_prev, c_prev, is_rnn, W_words, W_scales, 
             target = grouped[g][:].bitcast(F32)[:, half * HALF : (half + 1) * HALF, :, :]
             source = bank[:].rearrange("p j u r -> p j r u")
             if half == 0:
-                nc.scalar.copy(out=target, in_=source)
-            else:
                 nc.vector.tensor_copy(out=target, in_=source)
+            else:
+                nc.scalar.copy(out=target, in_=source)
 
         def quantise_xh(g):
             codes[g] = work.tile([P, GROUP_ROWS], U32, name="codes", align_bytes=64)
@@ -213,10 +213,13 @@ def tile_bag_lstm_pa_t_kernel(tc, x, h_prev, c_prev, is_rnn, W_words, W_scales, 
             if half == 1:
                 nc.sync.dma_start(out=c_rows[:, g * GROUP : (g + 1) * GROUP, :], in_=c_new[g][:])
 
-        XH_LEAD = 4
+        XH_LEAD = 3
         FO_LAG = 1
         IG_LAG = 3
         for step in range(-XH_LEAD, 2 * GROUPS + IG_LAG):
+            g, half = divmod(step + 1, 2)
+            if half == 0 and 0 <= g < GROUPS:
+                quantise_xh(g)
             g, part = divmod(step, 2)
             if part == 0 and 0 <= g - 1 < GROUPS:
                 multiply_i_g(g - 1)
@@ -225,9 +228,6 @@ def tile_bag_lstm_pa_t_kernel(tc, x, h_prev, c_prev, is_rnn, W_words, W_scales, 
             g, half = divmod(step - FO_LAG, 2)
             if 0 <= g < GROUPS:
                 blend_f_o(g, half)
-            g, half = divmod(step + XH_LEAD - 2, 2)
-            if half == 0 and 0 <= g < GROUPS:
-                quantise_xh(g)
             g, half = divmod(step - IG_LAG, 2)
             if 0 <= g < GROUPS:
                 finish_c(g, half)

@@ -49,7 +49,6 @@ def tile_bag_lstm_pa_t_kernel(tc, x, h_prev, c_prev, is_rnn, W_words, W_scales, 
         xh_psum = stack.enter_context(tc.psum_pool(name="xh_psum", bufs=1))
         fo_psum = stack.enter_context(tc.psum_pool(name="fo_psum", bufs=2))
         ig_psum = stack.enter_context(tc.psum_pool(name="ig_psum", bufs=1))
-        stack.enter_context(tc.manual_schedule())
 
         xh = {}
         c_old = {}

@@ -46,9 +46,7 @@ def tile_bag_lstm_pa_t_kernel(tc, x, h_prev, c_prev, is_rnn, W_words, W_scales, 
         work = stack.enter_context(tc.tile_pool(name="work", bufs=2))
         result = stack.enter_context(tc.tile_pool(name="result", bufs=3))
         gates_psum = stack.enter_context(tc.psum_pool(name="gates_psum", bufs=4))
-        xh_psum = stack.enter_context(tc.psum_pool(name="xh_psum", bufs=1))
-        fo_psum = stack.enter_context(tc.psum_pool(name="fo_psum", bufs=2))
-        ig_psum = stack.enter_context(tc.psum_pool(name="ig_psum", bufs=1))
+        turn_psum = stack.enter_context(tc.psum_pool(name="turn_psum", bufs=4))
 
         xh = {}
         c_old = {}
@@ -97,7 +95,7 @@ def tile_bag_lstm_pa_t_kernel(tc, x, h_prev, c_prev, is_rnn, W_words, W_scales, 
 
         b_rows_f32 = const.tile([P, P], F32)
         nc.vector.tensor_copy(out=b_rows_f32[:], in_=b_rows[:])
-        b_columns = ig_psum.tile([P, P], F32, tag="ig")
+        b_columns = turn_psum.tile([P, P], F32, tag="turn")
         nc.tensor.transpose(b_columns[:], b_rows_f32[:], ident[:])
         bias = const.tile([P, GATES // P], F32)
         nc.vector.tensor_copy(out=bias[:], in_=b_columns[:, 0 : GATES // P])
@@ -115,7 +113,7 @@ def tile_bag_lstm_pa_t_kernel(tc, x, h_prev, c_prev, is_rnn, W_words, W_scales, 
                     load_inputs(g + PREFETCH)
                 grouped[g] = work.tile([P, GROUP, P, 4], BF16, name="grouped", align_bytes=64)
             words = xh[g][:].bitcast(F32)
-            bank = xh_psum.tile([P, HALF, 2, P], F32, tag="xh_t")
+            bank = turn_psum.tile([P, HALF, 2, P], F32, tag="turn")
             for j in range(HALF):
                 for u in range(2):
                     nc.tensor.transpose(bank[:, j, u, :], words[:, half * HALF + j, u : K // 2 : 2], ident[:])
@@ -174,7 +172,7 @@ def tile_bag_lstm_pa_t_kernel(tc, x, h_prev, c_prev, is_rnn, W_words, W_scales, 
                 kept[g] = result.tile([P, GROUP, H], F32, name="kept")
             for j in range(half * HALF, (half + 1) * HALF):
                 t = g * GROUP + j
-                bank = fo_psum.tile([P, 2, H], F32, tag="fo")
+                bank = turn_psum.tile([P, 2, H], F32, tag="turn")
                 transpose_back(bank[:, 0, :], gate_t[g, GATE_F], j)
                 transpose_back(bank[:, 1, :], gate_t[g, GATE_O], j)
                 nc.vector.tensor_scalar(
@@ -195,7 +193,7 @@ def tile_bag_lstm_pa_t_kernel(tc, x, h_prev, c_prev, is_rnn, W_words, W_scales, 
         def finish_c(g, half):
             if half == 0:
                 c_new[g] = result.tile([P, GROUP, H], F32, name="c_new")
-            bank = ig_psum.tile([P, HALF, H], F32, tag="ig")
+            bank = turn_psum.tile([P, HALF, H], F32, tag="turn")
             for jj in range(HALF):
                 transpose_back(bank[:, jj, :], ig_t[g], half * HALF + jj)
             for jj in range(HALF):

@@ -158,7 +158,8 @@ def tile_bag_lstm_pa_t_kernel(tc, x, h_prev, c_prev, is_rnn, W_words, W_scales, 
 
         def multiply_i_g(g):
             ig_t[g] = work.tile([P, H_BLOCKS, GROUP_ROWS], F32, name="ig_t")
-            nc.gpsimd.tensor_tensor(out=ig_t[g][:], in0=gate_t[g, GATE_I][:], in1=gate_t[g, GATE_G][:], op=ALU.mult)
+            engine = nc.vector if g == GROUPS - 1 else nc.gpsimd
+            engine.tensor_tensor(out=ig_t[g][:], in0=gate_t[g, GATE_I][:], in1=gate_t[g, GATE_G][:], op=ALU.mult)
 
         def transpose_back(bank_columns, values_t, j):
             for hb in range(H_BLOCKS):
@@ -207,7 +208,10 @@ def tile_bag_lstm_pa_t_kernel(tc, x, h_prev, c_prev, is_rnn, W_words, W_scales, 
                     op0=ALU.mult,
                     op1=ALU.add,
                 )
-            if half == 1:
+            if g == GROUPS - 1:
+                first = g * GROUP + half * HALF
+                nc.sync.dma_start(out=c_rows[:, first : first + HALF, :], in_=c_new[g][:, half * HALF : (half + 1) * HALF, :])
+            elif half == 1:
                 nc.sync.dma_start(out=c_rows[:, g * GROUP : (g + 1) * GROUP, :], in_=c_new[g][:])
 
         XH_LEAD = 3

from contextlib import ExitStack

import concourse.mybir as mybir
from concourse.masks import make_identity

F32 = mybir.dt.float32
BF16 = mybir.dt.bfloat16
I32 = mybir.dt.int32
U32 = mybir.dt.uint32
U8 = mybir.dt.uint8
FP8X4 = mybir.dt.float8_e4m3fn_x4
FP4X4 = mybir.dt.float4_e2m1fn_x4
ACT = mybir.ActivationFunctionType
ALU = mybir.AluOpType

P = 128
B = 8192
H = 256
K = 2 * H
GATES = 4 * H
H_BLOCKS = H // P
GATE_I, GATE_F, GATE_G, GATE_O = 0, 1, 2, 3
ROW_TILES = B // P
GROUP = 4
GROUP_ROWS = GROUP * P
GROUPS = ROW_TILES // GROUP
HALF = GROUP // 2
PREFETCH = 3

FLOPS = 2 * B * K * GATES


def tile_bag_lstm_pa_t_kernel(tc, x, h_prev, c_prev, is_rnn, W_words, W_scales, b, out_0, out_1):
    nc = tc.nc

    x_rows = x.rearrange("(p t) k -> p t k", t=ROW_TILES)
    h_rows = h_prev.rearrange("(p t) k -> p t k", t=ROW_TILES)
    c_prev_rows = c_prev.rearrange("(p t) k -> p t k", t=ROW_TILES)
    c_rows = out_0.rearrange("(p t) k -> p t k", t=ROW_TILES)
    o_rows = out_1.rearrange("(p t) k -> p t k", t=ROW_TILES)

    with ExitStack() as stack:
        const = stack.enter_context(tc.tile_pool(name="const", bufs=1))
        xh_pool = stack.enter_context(tc.tile_pool(name="xh", bufs=PREFETCH + 2))
        c_prev_pool = stack.enter_context(tc.tile_pool(name="c_prev", bufs=PREFETCH + 5))
        work = stack.enter_context(tc.tile_pool(name="work", bufs=2))
        result = stack.enter_context(tc.tile_pool(name="result", bufs=3))
        gates_psum = stack.enter_context(tc.psum_pool(name="gates_psum", bufs=4))
        turn_psum = stack.enter_context(tc.psum_pool(name="turn_psum", bufs=4))

        xh = {}
        c_old = {}
        grouped = {}
        codes = {}
        scales = {}
        gate_t = {}
        ig_t = {}
        blend = {}
        kept = {}
        c_new = {}

        def load_inputs(g):
            tiles = slice(g * GROUP, (g + 1) * GROUP)
            xh[g] = xh_pool.tile([P, GROUP, K], BF16, name="xh")
            nc.sync.dma_start(out=xh[g][:, :, 0:H], in_=x_rows[:, tiles, :])
            nc.sync.dma_start(out=xh[g][:, :, H:K], in_=h_rows[:, tiles, :])
            c_old[g] = c_prev_pool.tile([P, GROUP, H], BF16, name="c_old")
            nc.sync.dma_start(out=c_old[g][:], in_=c_prev_rows[:, tiles, :])

        b_rows = const.tile([P, P], BF16)
        nc.vector.memset(b_rows[:], 0.0)
        nc.sync.dma_start(out=b_rows[0 : GATES // P, :], in_=b.rearrange("(r c) -> r c", c=P))
        m_bf16 = const.tile([P, ROW_TILES], BF16)
        nc.sync.dma_start(out=m_bf16[:], in_=is_rnn.rearrange("(p t) o -> p (t o)", t=ROW_TILES))
        load_inputs(0)

        w_words = const.tile([P, 2 * GATES], U8, align_bytes=64)
        nc.sync.dma_start(out=w_words[:].bitcast(I32), in_=W_words[0].bitcast(I32))
        w_scales = const.tile([P, GATES], U8, align_bytes=64)
        nc.vector.memset(w_scales[:].bitcast(I32), 0)
        for quadrant in range(4):
            nc.sync.dma_start(
                out=w_scales[32 * quadrant : 32 * quadrant + 4, :].bitcast(I32),
                in_=W_scales[0, 4 * quadrant : 4 * quadrant + 4, :].bitcast(I32),
            )
        for g in range(1, PREFETCH):
            load_inputs(g)

        ident = const.tile([P, P], F32)
        make_identity(nc, ident[:])

        warm = const.tile([P, 1], F32)
        nc.vector.memset(warm[:], 0.0)
        nc.scalar.activation(out=warm[:], in_=warm[:], func=ACT.Sigmoid)

        b_rows_f32 = const.tile([P, P], F32)
        nc.vector.tensor_copy(out=b_rows_f32[:], in_=b_rows[:])
        b_columns = turn_psum.tile([P, P], F32, tag="turn")
        nc.tensor.transpose(b_columns[:], b_rows_f32[:], ident[:])
        bias = const.tile([P, GATES // P], F32)
        nc.vector.tensor_copy(out=bias[:], in_=b_columns[:, 0 : GATES // P])

        m = const.tile([P, ROW_TILES], F32)
        nc.vector.tensor_copy(out=m[:], in_=m_bf16[:])
        one_minus_m = const.tile([P, ROW_TILES], F32)
        nc.vector.tensor_scalar(
            out=one_minus_m[:], in0=m_bf16[:], scalar1=-1.0, scalar2=1.0, op0=ALU.mult, op1=ALU.add
        )

        def transpose_xh(g, half):
            if half == 0:
                if g + PREFETCH < GROUPS:
                    load_inputs(g + PREFETCH)
                grouped[g] = work.tile([P, GROUP, P, 4], BF16, name="grouped", align_bytes=64)
            words = xh[g][:].bitcast(F32)
            bank = turn_psum.tile([P, HALF, 2, P], F32, tag="turn")
            for j in range(HALF):
                for u in range(2):
                    nc.tensor.transpose(bank[:, j, u, :], words[:, half * HALF + j, u : K // 2 : 2], ident[:])
            target = grouped[g][:].bitcast(F32)[:, half * HALF : (half + 1) * HALF, :, :]
            source = bank[:].rearrange("p j u r -> p j r u")
            if half == 0:
                nc.vector.tensor_copy(out=target, in_=source)
            else:
                nc.scalar.copy(out=target, in_=source)

        def quantise_xh(g):
            codes[g] = work.tile([P, GROUP_ROWS], U32, name="codes", align_bytes=64)
            scales[g] = work.tile([P, GROUP_ROWS], U8, name="scales", align_bytes=64)
            nc.vector.quantize_mx(
                out=codes[g][:].bitcast(FP8X4),
                scales=scales[g][:],
                in_=grouped[g][:].rearrange("p j r t -> p (j r t)"),
            )

        def compute_gates(g, gates):
            for gate in gates:
                gate_t[g, gate] = work.tile([P, H_BLOCKS, GROUP_ROWS], F32, name="gate_t%d" % gate)
                for hb in range(H_BLOCKS):
                    block = gate * H_BLOCKS + hb
                    sums = gates_psum.tile([P, GROUP_ROWS], F32, tag="sums")
                    nc.tensor.matmul_mx(
                        out=sums[:],
                        lhsT=w_words[:, 2 * P * block : 2 * P * (block + 1)].bitcast(FP4X4),
                        lhsT_scale=w_scales[:, P * block : P * (block + 1)],
                        rhs=codes[g][:].bitcast(FP8X4),
                        rhs_scale=scales[g][:],
                        start=True,
                        stop=True,
                    )
                    nc.scalar.activation(
                        out=gate_t[g, gate][:, hb, :],
                        in_=sums[:],
                        func=ACT.Tanh if gate == GATE_G else ACT.Sigmoid,
                        bias=bias[:, block : block + 1],
                        scale=1.0,
                    )

        def multiply_i_g(g):
            ig_t[g] = work.tile([P, H_BLOCKS, GROUP_ROWS], F32, name="ig_t")
            engine = nc.vector if g == GROUPS - 1 else nc.gpsimd
            engine.tensor_tensor(out=ig_t[g][:], in0=gate_t[g, GATE_I][:], in1=gate_t[g, GATE_G][:], op=ALU.mult)

        def transpose_back(bank_columns, values_t, j):
            for hb in range(H_BLOCKS):
                nc.tensor.transpose(
                    bank_columns[:, hb * P : (hb + 1) * P], values_t[:, hb, j * P : (j + 1) * P], ident[:]
                )

        def blend_f_o(g, half):
            if half == 0:
                blend[g] = result.tile([P, 2, GROUP, H], F32, name="blend")
                kept[g] = result.tile([P, GROUP, H], F32, name="kept")
            for j in range(half * HALF, (half + 1) * HALF):
                t = g * GROUP + j
                bank = turn_psum.tile([P, 2, H], F32, tag="turn")
                transpose_back(bank[:, 0, :], gate_t[g, GATE_F], j)
                transpose_back(bank[:, 1, :], gate_t[g, GATE_O], j)
                nc.vector.tensor_scalar(
                    out=blend[g][:, :, j, :],
                    in0=bank[:],
                    scalar1=m[:, t : t + 1],
                    scalar2=one_minus_m[:, t : t + 1],
                    op0=ALU.mult,
                    op1=ALU.add,
                )
            tiles = slice(half * HALF, (half + 1) * HALF)
            nc.gpsimd.tensor_tensor(
                out=kept[g][:, tiles, :], in0=blend[g][:, 0, tiles, :], in1=c_old[g][:, tiles, :], op=ALU.mult
            )
            if half == 1:
                nc.sync.dma_start(out=o_rows[:, g * GROUP : (g + 1) * GROUP, :], in_=blend[g][:, 1, :, :])

        def finish_c(g, half):
            if half == 0:
                c_new[g] = result.tile([P, GROUP, H], F32, name="c_new")
            bank = turn_psum.tile([P, HALF, H], F32, tag="turn")
            for jj in range(HALF):
                transpose_back(bank[:, jj, :], ig_t[g], half * HALF + jj)
            for jj in range(HALF):
                j = half * HALF + jj
                t = g * GROUP + j
                nc.vector.scalar_tensor_tensor(
                    out=c_new[g][:, j, :],
                    in0=bank[:, jj, :],
                    scalar=m[:, t : t + 1],
                    in1=kept[g][:, j, :],
                    op0=ALU.mult,
                    op1=ALU.add,
                )
            if g == GROUPS - 1:
                first = g * GROUP + half * HALF
                nc.sync.dma_start(out=c_rows[:, first : first + HALF, :], in_=c_new[g][:, half * HALF : (half + 1) * HALF, :])
            elif half == 1:
                nc.sync.dma_start(out=c_rows[:, g * GROUP : (g + 1) * GROUP, :], in_=c_new[g][:])

        XH_LEAD = 3
        FO_LAG = 1
        IG_LAG = 3
        for step in range(-XH_LEAD, 2 * GROUPS + IG_LAG):
            g, half = divmod(step + 1, 2)
            if half == 0 and 0 <= g < GROUPS:
                quantise_xh(g)
            g, part = divmod(step, 2)
            if part == 0 and 0 <= g - 1 < GROUPS:
                multiply_i_g(g - 1)
            if 0 <= g < GROUPS:
                compute_gates(g, (GATE_F, GATE_O) if part == 0 else (GATE_I, GATE_G))
            g, half = divmod(step - FO_LAG, 2)
            if 0 <= g < GROUPS:
                blend_f_o(g, half)
            g, half = divmod(step - IG_LAG, 2)
            if 0 <= g < GROUPS:
                finish_c(g, half)
            g, half = divmod(step + XH_LEAD, 2)
            if 0 <= g < GROUPS:
                transpose_xh(g, half)
